import numpy as np
import ml_dtypes


def mxq(x, axis, fmt="e4m3"):
    dtype, down = {"e4m3": (ml_dtypes.float8_e4m3fn, 7), "e5m2": (ml_dtypes.float8_e5m2, 14)}[fmt]
    v = np.moveaxis(np.asarray(x, np.float32).astype(ml_dtypes.bfloat16).astype(np.float64), axis, -1)
    blocks = v.reshape(v.shape[:-1] + (-1, 32))
    amax = np.abs(blocks).max(-1, keepdims=True)
    byte = np.maximum(np.where(amax > 0, np.frexp(amax)[1] - 1 + 127, 0) - down, 1)
    scale = np.exp2(byte - 127.0)
    codes = (blocks / scale).astype(np.float32).astype(dtype).astype(np.float64)
    return np.moveaxis((codes * scale).reshape(v.shape), -1, axis)


WIDE = False


def mx_kscale(k):
    if not WIDE:
        return np.ones(k)
    levels = np.array([10, -10, 5, -5, 0])
    a = np.random.permutation(np.resize(levels, k // 512 * 4)).reshape(k // 512, 4)
    idx = np.arange(k)
    return np.exp2(a[idx // 512, idx % 128 // 32])


BF16 = ml_dtypes.bfloat16


def bf(x):
    return np.asarray(x, np.float32).astype(BF16)


def f64(x):
    return np.asarray(x).astype(np.float64)


B, CH, C1, C2, D, NF, W, H = 2, 1024, 128, 256, 2, 16, 16, 16
N = NF * W * H
M = NF * (W // D) * (H // D)


def conv(xq, w, b):
    return (mxq(f64(w), 1, "e4m3") @ xq) + f64(b)[None, :, None]


def maxpool_wh(v):
    return v.reshape(B, -1, NF, W // D, D, H // D, D).max(axis=(4, 6)).reshape(B, -1, M)


def setup_inputs():
    s = mx_kscale(CH)
    return {"x": bf(np.random.standard_normal((B, CH, NF, W, H)) * s[None, :, None, None, None]),
            "w_theta": bf(np.random.standard_normal((C1, CH)) * 0.3 / np.sqrt(CH) / s),
            "b_theta": bf(np.random.standard_normal(C1) * 0.1),
            "w_phi": bf(np.random.standard_normal((C1, CH)) * 0.3 / np.sqrt(CH) / s),
            "b_phi": bf(np.random.standard_normal(C1) * 0.1),
            "w_g": bf(np.random.standard_normal((C2, CH)) / np.sqrt(CH) / s),
            "b_g": bf(np.random.standard_normal(C2) * 0.2)}


def reference(x, w_theta, b_theta, w_phi, b_phi, w_g, b_g):
    xq = mxq(f64(x).reshape(B, CH, N), 1, "e4m3")
    theta = np.tanh(conv(xq, w_theta, b_theta)).transpose(0, 2, 1)
    phi = maxpool_wh(np.tanh(conv(xq, w_phi, b_phi))).transpose(0, 2, 1)
    g = maxpool_wh(conv(xq, w_g, b_g)).transpose(0, 2, 1)
    return theta, phi, g

@@ -1,0 +1,233 @@
+from contextlib import ExitStack
+
+import concourse.mybir as mybir
+from concourse.masks import make_identity
+
+BF16 = mybir.dt.bfloat16
+F32 = mybir.dt.float32
+U32 = mybir.dt.uint32
+U8 = mybir.dt.uint8
+FP8X4 = mybir.dt.float8_e4m3fn_x4
+ACT = mybir.ActivationFunctionType
+
+P = 128
+PACK = 4
+K_PASS = P * PACK
+BATCH = 2
+CH = 1024
+PASSES = CH // K_PASS
+LOCS = 16 * 16 * 16
+SLAB = 1024
+CHUNK = 512
+CHUNKS = SLAB // CHUNK
+SLABS = BATCH * LOCS // SLAB
+SLABS_PER_BATCH = LOCS // SLAB
+OUT_TILES = 4
+POOLED_TILES = 3
+POOLED = SLAB // 4
+V_COLS = 576
+
+FLOPS = 2 * BATCH * LOCS * CH * OUT_TILES * P
+
+
+def tile_selfattention3d_pb_t_kernel(
+    tc, x, w_theta, b_theta, w_phi, b_phi, w_g, b_g, out_0, out_1, out_2
+):
+    nc = tc.nc
+    x_view = x.rearrange("b (g t p) f i j -> b g p t (f i j)", g=PASSES, t=PACK, p=P)
+
+    with ExitStack() as ctx:
+        consts = ctx.enter_context(tc.tile_pool(name="consts", bufs=1))
+        raw_pool = ctx.enter_context(tc.tile_pool(name="raw", bufs=6))
+        grouped_pool = ctx.enter_context(tc.tile_pool(name="grouped", bufs=4))
+        mx_pool = ctx.enter_context(tc.tile_pool(name="mx", bufs=3))
+        work = ctx.enter_context(tc.tile_pool(name="work", bufs=3))
+        psum_acc = ctx.enter_context(tc.psum_pool(name="psum_acc", bufs=5))
+        psum_tr = ctx.enter_context(tc.psum_pool(name="psum_tr", bufs=3))
+
+        ident_bf = consts.tile([P, P], BF16)
+        make_identity(nc, ident_bf[:])
+        ident_f32 = consts.tile([P, P], F32)
+        make_identity(nc, ident_f32[:])
+
+        w_rows = consts.tile([P, OUT_TILES, CH], BF16)
+        nc.sync.dma_start(out=w_rows[:, 0, :], in_=w_theta)
+        nc.sync.dma_start(out=w_rows[:, 1, :], in_=w_phi)
+        nc.sync.dma_start(out=w_rows[:, 2:4, :], in_=w_g.rearrange("(h o) k -> o h k", h=2))
+
+        bias_rows = consts.tile([P, P], BF16)
+        nc.vector.memset(bias_rows[:], 0.0)
+        nc.scalar.dma_start(out=bias_rows[0:1, :], in_=b_theta.rearrange("(h c) -> h c", h=1))
+        nc.scalar.dma_start(out=bias_rows[1:2, :], in_=b_phi.rearrange("(h c) -> h c", h=1))
+        nc.scalar.dma_start(out=bias_rows[2:4, :], in_=b_g.rearrange("(h c) -> h c", h=2))
+
+        raw = {}
+
+        def load(s):
+            bt, n0 = s // SLABS_PER_BATCH, (s % SLABS_PER_BATCH) * SLAB
+            for g in range(PASSES):
+                rows = raw_pool.tile([P, PACK, SLAB], BF16, name="rows")
+                nc.sync.dma_start(out=rows[:], in_=x_view[bt, g, :, :, n0 : n0 + SLAB])
+                raw[(s, g)] = rows
+
+        load(0)
+        load(1)
+
+        w_grouped = consts.tile([P, PASSES, OUT_TILES * P, PACK], BF16, align_bytes=64)
+        w_codes = consts.tile([P, PASSES, OUT_TILES * P], U32, align_bytes=64)
+        w_scales = consts.tile([P, PASSES, OUT_TILES * P], U8, align_bytes=64)
+        for g in range(PASSES):
+            for h in range(2):
+                w_t = psum_tr.tile([P, 2, PACK, P], BF16, tag="tr")
+                for o in range(2):
+                    for t in range(PACK):
+                        k0 = g * K_PASS + t * P
+                        nc.tensor.transpose(
+                            w_t[:, o, t, :], w_rows[:, 2 * h + o, k0 : k0 + P], ident_bf[:]
+                        )
+                dst = w_grouped[:, g, 2 * h * P : (2 * h + 2) * P, :].rearrange(
+                    "p (o r) t -> p o r t", o=2
+                )
+                src = w_t[:].rearrange("p o t r -> p o r t")
+                if h == 0:
+                    nc.vector.tensor_copy(out=dst, in_=src)
+                else:
+                    nc.scalar.copy(out=dst, in_=src)
+        for g in range(PASSES):
+            nc.vector.quantize_mx(
+                out=w_codes[:, g, :].bitcast(FP8X4),
+                scales=w_scales[:, g, :],
+                in_=w_grouped[:, g, :, :].rearrange("p r t -> p (r t)"),
+            )
+
+        bias_t = psum_tr.tile([P, P], BF16, tag="tr")
+        nc.tensor.transpose(bias_t[:], bias_rows[:], ident_bf[:])
+        bias_col = consts.tile([P, OUT_TILES], F32)
+        nc.vector.tensor_copy(out=bias_col[:], in_=bias_t[:, 0:OUT_TILES])
+
+        x_codes = {}
+        x_scales = {}
+        theta_act = {}
+        pooled = {}
+        pooled_act = {}
+
+        def quantise(s):
+            codes = mx_pool.tile([P, PASSES, SLAB], U32, align_bytes=64, name="codes")
+            scales = mx_pool.tile([P, PASSES, SLAB], U8, align_bytes=64, name="scales")
+            grouped = []
+            for g in range(PASSES):
+                quads = grouped_pool.tile([P, SLAB, PACK], BF16, align_bytes=64, name="quads")
+                dst = quads[:].rearrange("p (c i) t -> p c t i", i=4)
+                src = raw[(s, g)][:].rearrange("p t (c i) -> p c t i", i=4)
+                cut = V_COLS // 4
+                nc.vector.tensor_copy(out=dst[:, :cut], in_=src[:, :cut])
+                nc.scalar.copy(out=dst[:, cut:], in_=src[:, cut:])
+                grouped.append(quads)
+            for g in range(PASSES):
+                nc.vector.quantize_mx(
+                    out=codes[:, g, :].bitcast(FP8X4),
+                    scales=scales[:, g, :],
+                    in_=grouped[g][:].rearrange("p n t -> p (n t)"),
+                )
+            x_codes[s] = codes
+            x_scales[s] = scales
+
+        def convolve(s, u):
+            cols = slice(u * CHUNK, (u + 1) * CHUNK)
+            if u == 0:
+                pooled[s] = work.tile([P, POOLED_TILES, POOLED], F32, name="pooled_max")
+            for o in range(OUT_TILES):
+                outs = slice(o * P, (o + 1) * P)
+                acc = psum_acc.tile([P, CHUNK], F32)
+                for g in range(PASSES):
+                    nc.tensor.matmul_mx(
+                        out=acc[:],
+                        lhsT=w_codes[:, g, outs].bitcast(FP8X4),
+                        lhsT_scale=w_scales[:, g, outs],
+                        rhs=x_codes[s][:, g, cols].bitcast(FP8X4),
+                        rhs_scale=x_scales[s][:, g, cols],
+                        start=(g == 0),
+                        stop=(g == PASSES - 1),
+                    )
+                if o == 0:
+                    th = work.tile([P, 4, P], F32, name="th")
+                    nc.scalar.activation(
+                        out=th[:],
+                        in_=acc[:].rearrange("p (q r) -> p r q", r=4),
+                        func=ACT.Tanh,
+                        bias=bias_col[:, 0:1],
+                    )
+                    theta_act[(s, u)] = th
+                else:
+                    nc.vector.tensor_reduce(
+                        out=pooled[s][:, o - 1, u * P : (u + 1) * P].rearrange(
+                            "p (r j) -> p r j", j=8
+                        ),
+                        in_=acc[:].rearrange("p (r a j b) -> p r j a b", a=2, j=8, b=2),
+                        axis=mybir.AxisListType.XY,
+                        op=mybir.AluOpType.max,
+                    )
+
+        def store_theta(s, u):
+            bt = s // SLABS_PER_BATCH
+            n0 = (s % SLABS_PER_BATCH) * SLAB + u * CHUNK
+            th_t = psum_tr.tile([P, 4, P], F32, tag="tr")
+            for r in range(4):
+                nc.tensor.transpose(th_t[:, r, :], theta_act[(s, u)][:, r, :], ident_f32[:])
+            th_out = work.tile([P, 4, P], F32)
+            nc.scalar.copy(out=th_out[:], in_=th_t[:])
+            nc.sync.dma_start(
+                out=out_0[bt, n0 : n0 + CHUNK, :].rearrange("(q r) c -> q r c", r=4),
+                in_=th_out[:],
+            )
+
+        def activate_pooled(s):
+            acted = work.tile([P, POOLED_TILES, 2, P], F32)
+            for o in range(POOLED_TILES):
+                nc.scalar.activation(
+                    out=acted[:, o, :, :],
+                    in_=pooled[s][:, o, :].rearrange("p (q r) -> p r q", r=2),
+                    func=(ACT.Tanh if o == 0 else ACT.Identity),
+                    bias=bias_col[:, o + 1 : o + 2],
+                )
+            pooled_act[s] = acted
+
+        def store_pooled(s):
+            bt = s // SLABS_PER_BATCH
+            m0 = (s % SLABS_PER_BATCH) * POOLED
+            phi_t = psum_tr.tile([P, 2, P], F32, tag="tr")
+            g_t = psum_tr.tile([P, 2, 2, P], F32, tag="tr")
+            for r in range(2):
+                nc.tensor.transpose(phi_t[:, r, :], pooled_act[s][:, 0, r, :], ident_f32[:])
+                for h in range(2):
+                    nc.tensor.transpose(
+                        g_t[:, r, h, :], pooled_act[s][:, 1 + h, r, :], ident_f32[:]
+                    )
+            phi_out = work.tile([P, 2, P], F32)
+            nc.scalar.copy(out=phi_out[:], in_=phi_t[:])
+            g_out = work.tile([P, 2, 2 * P], F32)
+            nc.scalar.copy(out=g_out[:], in_=g_t[:].rearrange("p r h c -> p r (h c)"))
+            nc.sync.dma_start(
+                out=out_1[bt, m0 : m0 + POOLED, :].rearrange("(q r) c -> q r c", r=2),
+                in_=phi_out[:],
+            )
+            nc.sync.dma_start(
+                out=out_2[bt, m0 : m0 + POOLED, :].rearrange("(q r) c -> q r c", r=2),
+                in_=g_out[:],
+            )
+
+        quantise(0)
+        for s in range(SLABS + 1):
+            if s + 2 < SLABS:
+                load(s + 2)
+            if s + 1 < SLABS:
+                quantise(s + 1)
+            if s < SLABS:
+                convolve(s, 0)
+            if s > 0:
+                store_theta(s - 1, 1)
+                store_pooled(s - 1)
+            if s < SLABS:
+                convolve(s, 1)
+                store_theta(s, 0)
+                activate_pooled(s)

@@ -19,13 +19,16 @@ PASSES = CH // K_PASS
 LOCS = 16 * 16 * 16
 SLAB = 1024
 CHUNK = 512
-CHUNKS = SLAB // CHUNK
-SLABS = BATCH * LOCS // SLAB
 SLABS_PER_BATCH = LOCS // SLAB
+X_TILES = BATCH * SLABS_PER_BATCH * PASSES
+CHUNKS = BATCH * LOCS // CHUNK
 OUT_TILES = 4
 POOLED_TILES = 3
+THETA = 3
 POOLED = SLAB // 4
-V_COLS = 576
+V_COLS = 528
+
+LOADS_AHEAD = 6
 
 FLOPS = 2 * BATCH * LOCS * CH * OUT_TILES * P
 
@@ -39,98 +42,46 @@ def tile_selfattention3d_pb_t_kernel(
     with ExitStack() as ctx:
         consts = ctx.enter_context(tc.tile_pool(name="consts", bufs=1))
         raw_pool = ctx.enter_context(tc.tile_pool(name="raw", bufs=6))
-        grouped_pool = ctx.enter_context(tc.tile_pool(name="grouped", bufs=4))
-        mx_pool = ctx.enter_context(tc.tile_pool(name="mx", bufs=3))
+        grouped_pool = ctx.enter_context(tc.tile_pool(name="grouped", bufs=3))
+        mx_pool = ctx.enter_context(tc.tile_pool(name="mx", bufs=6))
         work = ctx.enter_context(tc.tile_pool(name="work", bufs=3))
         psum_acc = ctx.enter_context(tc.psum_pool(name="psum_acc", bufs=5))
         psum_tr = ctx.enter_context(tc.psum_pool(name="psum_tr", bufs=3))
 
-        ident_bf = consts.tile([P, P], BF16)
-        make_identity(nc, ident_bf[:])
-        ident_f32 = consts.tile([P, P], F32)
-        make_identity(nc, ident_f32[:])
-
-        w_rows = consts.tile([P, OUT_TILES, CH], BF16)
-        nc.sync.dma_start(out=w_rows[:, 0, :], in_=w_theta)
-        nc.sync.dma_start(out=w_rows[:, 1, :], in_=w_phi)
-        nc.sync.dma_start(out=w_rows[:, 2:4, :], in_=w_g.rearrange("(h o) k -> o h k", h=2))
-
-        bias_rows = consts.tile([P, P], BF16)
-        nc.vector.memset(bias_rows[:], 0.0)
-        nc.scalar.dma_start(out=bias_rows[0:1, :], in_=b_theta.rearrange("(h c) -> h c", h=1))
-        nc.scalar.dma_start(out=bias_rows[1:2, :], in_=b_phi.rearrange("(h c) -> h c", h=1))
-        nc.scalar.dma_start(out=bias_rows[2:4, :], in_=b_g.rearrange("(h c) -> h c", h=2))
-
         raw = {}
-
-        def load(s):
-            bt, n0 = s // SLABS_PER_BATCH, (s % SLABS_PER_BATCH) * SLAB
-            for g in range(PASSES):
-                rows = raw_pool.tile([P, PACK, SLAB], BF16, name="rows")
-                nc.sync.dma_start(out=rows[:], in_=x_view[bt, g, :, :, n0 : n0 + SLAB])
-                raw[(s, g)] = rows
-
-        load(0)
-        load(1)
-
-        w_grouped = consts.tile([P, PASSES, OUT_TILES * P, PACK], BF16, align_bytes=64)
-        w_codes = consts.tile([P, PASSES, OUT_TILES * P], U32, align_bytes=64)
-        w_scales = consts.tile([P, PASSES, OUT_TILES * P], U8, align_bytes=64)
-        for g in range(PASSES):
-            for h in range(2):
-                w_t = psum_tr.tile([P, 2, PACK, P], BF16, tag="tr")
-                for o in range(2):
-                    for t in range(PACK):
-                        k0 = g * K_PASS + t * P
-                        nc.tensor.transpose(
-                            w_t[:, o, t, :], w_rows[:, 2 * h + o, k0 : k0 + P], ident_bf[:]
-                        )
-                dst = w_grouped[:, g, 2 * h * P : (2 * h + 2) * P, :].rearrange(
-                    "p (o r) t -> p o r t", o=2
-                )
-                src = w_t[:].rearrange("p o t r -> p o r t")
-                if h == 0:
-                    nc.vector.tensor_copy(out=dst, in_=src)
-                else:
-                    nc.scalar.copy(out=dst, in_=src)
-        for g in range(PASSES):
-            nc.vector.quantize_mx(
-                out=w_codes[:, g, :].bitcast(FP8X4),
-                scales=w_scales[:, g, :],
-                in_=w_grouped[:, g, :, :].rearrange("p r t -> p (r t)"),
-            )
-
-        bias_t = psum_tr.tile([P, P], BF16, tag="tr")
-        nc.tensor.transpose(bias_t[:], bias_rows[:], ident_bf[:])
-        bias_col = consts.tile([P, OUT_TILES], F32)
-        nc.vector.tensor_copy(out=bias_col[:], in_=bias_t[:, 0:OUT_TILES])
-
+        grouped = {}
         x_codes = {}
         x_scales = {}
         theta_act = {}
         pooled = {}
         pooled_act = {}
 
-        def quantise(s):
-            codes = mx_pool.tile([P, PASSES, SLAB], U32, align_bytes=64, name="codes")
-            scales = mx_pool.tile([P, PASSES, SLAB], U8, align_bytes=64, name="scales")
-            grouped = []
-            for g in range(PASSES):
-                quads = grouped_pool.tile([P, SLAB, PACK], BF16, align_bytes=64, name="quads")
-                dst = quads[:].rearrange("p (c i) t -> p c t i", i=4)
-                src = raw[(s, g)][:].rearrange("p t (c i) -> p c t i", i=4)
-                cut = V_COLS // 4
-                nc.vector.tensor_copy(out=dst[:, :cut], in_=src[:, :cut])
-                nc.scalar.copy(out=dst[:, cut:], in_=src[:, cut:])
-                grouped.append(quads)
-            for g in range(PASSES):
-                nc.vector.quantize_mx(
-                    out=codes[:, g, :].bitcast(FP8X4),
-                    scales=scales[:, g, :],
-                    in_=grouped[g][:].rearrange("p n t -> p (n t)"),
-                )
-            x_codes[s] = codes
-            x_scales[s] = scales
+        def load(j):
+            s, g = j // PASSES, j % PASSES
+            bt, n0 = s // SLABS_PER_BATCH, (s % SLABS_PER_BATCH) * SLAB
+            rows = raw_pool.tile([P, PACK, SLAB], BF16)
+            nc.sync.dma_start(out=rows[:], in_=x_view[bt, g, :, :, n0 : n0 + SLAB])
+            raw[j] = rows
+
+        def regroup(j):
+            quads = grouped_pool.tile([P, SLAB, PACK], BF16, align_bytes=64)
+            dst = quads[:].rearrange("p (c i) t -> p c t i", i=4)
+            src = raw[j][:].rearrange("p t (c i) -> p c t i", i=4)
+            v_end = V_COLS // 4
+            nc.vector.tensor_copy(out=dst[:, :v_end], in_=src[:, :v_end])
+            nc.scalar.copy(out=dst[:, v_end:], in_=src[:, v_end:])
+            grouped[j] = quads
+
+        def quantise(j):
+            codes = mx_pool.tile([P, SLAB], U32, align_bytes=64)
+            scales = mx_pool.tile([P, SLAB], U8, align_bytes=64)
+            nc.vector.quantize_mx(
+                out=codes[:].bitcast(FP8X4),
+                scales=scales[:],
+                in_=grouped[j][:].rearrange("p n t -> p (n t)"),
+            )
+            x_codes[j] = codes
+            x_scales[j] = scales
 
         def convolve(s, u):
             cols = slice(u * CHUNK, (u + 1) * CHUNK)
@@ -144,29 +95,29 @@ def tile_selfattention3d_pb_t_kernel(
                         out=acc[:],
                         lhsT=w_codes[:, g, outs].bitcast(FP8X4),
                         lhsT_scale=w_scales[:, g, outs],
-                        rhs=x_codes[s][:, g, cols].bitcast(FP8X4),
-                        rhs_scale=x_scales[s][:, g, cols],
+                        rhs=x_codes[PASSES * s + g][:, cols].bitcast(FP8X4),
+                        rhs_scale=x_scales[PASSES * s + g][:, cols],
                         start=(g == 0),
                         stop=(g == PASSES - 1),
                     )
-                if o == 0:
-                    th = work.tile([P, 4, P], F32, name="th")
-                    nc.scalar.activation(
-                        out=th[:],
-                        in_=acc[:].rearrange("p (q r) -> p r q", r=4),
-                        func=ACT.Tanh,
-                        bias=bias_col[:, 0:1],
-                    )
-                    theta_act[(s, u)] = th
-                else:
+                if o < POOLED_TILES:
                     nc.vector.tensor_reduce(
-                        out=pooled[s][:, o - 1, u * P : (u + 1) * P].rearrange(
+                        out=pooled[s][:, o, u * P : (u + 1) * P].rearrange(
                             "p (r j) -> p r j", j=8
                         ),
                         in_=acc[:].rearrange("p (r a j b) -> p r j a b", a=2, j=8, b=2),
                         axis=mybir.AxisListType.XY,
                         op=mybir.AluOpType.max,
                     )
+                else:
+                    th = work.tile([P, 4, P], F32, name="th")
+                    nc.scalar.activation(
+                        out=th[:],
+                        in_=acc[:].rearrange("p (q r) -> p r q", r=4),
+                        func=ACT.Tanh,
+                        bias=bias_col[:, THETA : THETA + 1],
+                    )
+                    theta_act[(s, u)] = th
 
         def store_theta(s, u):
             bt = s // SLABS_PER_BATCH
@@ -188,7 +139,7 @@ def tile_selfattention3d_pb_t_kernel(
                     out=acted[:, o, :, :],
                     in_=pooled[s][:, o, :].rearrange("p (q r) -> p r q", r=2),
                     func=(ACT.Tanh if o == 0 else ACT.Identity),
-                    bias=bias_col[:, o + 1 : o + 2],
+                    bias=bias_col[:, o : o + 1],
                 )
             pooled_act[s] = acted
 
@@ -216,18 +167,76 @@ def tile_selfattention3d_pb_t_kernel(
                 in_=g_out[:],
             )
 
+        load(0)
+        load(1)
+        w_rows = consts.tile([P, OUT_TILES, CH], BF16)
+        nc.sync.dma_start(out=w_rows[:, 0, :], in_=w_phi)
+        nc.sync.dma_start(out=w_rows[:, 1:3, :], in_=w_g.rearrange("(h o) k -> o h k", h=2))
+        nc.sync.dma_start(out=w_rows[:, THETA, :], in_=w_theta)
+        for j in range(2, LOADS_AHEAD):
+            load(j)
+
+        bias_rows = consts.tile([P, P], BF16)
+        nc.vector.memset(bias_rows[:], 0.0)
+        nc.scalar.dma_start(out=bias_rows[0:1, :], in_=b_phi.rearrange("(h c) -> h c", h=1))
+        nc.scalar.dma_start(out=bias_rows[1:3, :], in_=b_g.rearrange("(h c) -> h c", h=2))
+        nc.scalar.dma_start(
+            out=bias_rows[THETA : THETA + 1, :], in_=b_theta.rearrange("(h c) -> h c", h=1)
+        )
+        ident_bf = consts.tile([P, P], BF16)
+        make_identity(nc, ident_bf[:])
+        ident_f32 = consts.tile([P, P], F32)
+        make_identity(nc, ident_f32[:])
+
+        regroup(0)
+        regroup(1)
+
+        w_grouped = consts.tile([P, PASSES, OUT_TILES * P, PACK], BF16, align_bytes=64)
+        w_codes = consts.tile([P, PASSES, OUT_TILES * P], U32, align_bytes=64)
+        w_scales = consts.tile([P, PASSES, OUT_TILES * P], U8, align_bytes=64)
+        for g in range(PASSES):
+            for h in range(2):
+                w_t = psum_tr.tile([P, 2, PACK, P], BF16, tag="tr")
+                for o in range(2):
+                    for t in range(PACK):
+                        k0 = g * K_PASS + t * P
+                        nc.tensor.transpose(
+                            w_t[:, o, t, :], w_rows[:, 2 * h + o, k0 : k0 + P], ident_bf[:]
+                        )
+                dst = w_grouped[:, g, 2 * h * P : (2 * h + 2) * P, :].rearrange(
+                    "p (o r) t -> p o r t", o=2
+                )
+                src = w_t[:].rearrange("p o t r -> p o r t")
+                if h == 0:
+                    nc.vector.tensor_copy(out=dst, in_=src)
+                else:
+                    nc.scalar.copy(out=dst, in_=src)
+        bias_t = psum_tr.tile([P, P], BF16, tag="tr")
+        nc.tensor.transpose(bias_t[:], bias_rows[:], ident_bf[:])
+        bias_col = consts.tile([P, OUT_TILES], F32)
+        nc.vector.tensor_copy(out=bias_col[:], in_=bias_t[:, 0:OUT_TILES])
+        for g in range(PASSES):
+            nc.vector.quantize_mx(
+                out=w_codes[:, g, :].bitcast(FP8X4),
+                scales=w_scales[:, g, :],
+                in_=w_grouped[:, g, :, :].rearrange("p r t -> p (r t)"),
+            )
         quantise(0)
-        for s in range(SLABS + 1):
-            if s + 2 < SLABS:
-                load(s + 2)
-            if s + 1 < SLABS:
-                quantise(s + 1)
-            if s < SLABS:
-                convolve(s, 0)
-            if s > 0:
-                store_theta(s - 1, 1)
-                store_pooled(s - 1)
-            if s < SLABS:
-                convolve(s, 1)
-                store_theta(s, 0)
-                activate_pooled(s)
+        regroup(2)
+        quantise(1)
+
+        for h in range(CHUNKS + 1):
+            if h + LOADS_AHEAD < X_TILES:
+                load(h + LOADS_AHEAD)
+            if h + 3 < X_TILES:
+                regroup(h + 3)
+            if h + 2 < X_TILES:
+                quantise(h + 2)
+            if h < CHUNKS:
+                convolve(h // 2, h % 2)
+            if h > 0:
+                store_theta((h - 1) // 2, (h - 1) % 2)
+                if h % 2 == 0:
+                    store_pooled((h - 1) // 2)
+            if h % 2 == 1:
+                activate_pooled(h // 2)

@@ -26,7 +26,8 @@ OUT_TILES = 4
 POOLED_TILES = 3
 THETA = 3
 POOLED = SLAB // 4
-V_COLS = 528
+V_COLS = 360
+G_COLS = 256
 
 LOADS_AHEAD = 6
 
@@ -68,8 +69,17 @@ def tile_selfattention3d_pb_t_kernel(
             dst = quads[:].rearrange("p (c i) t -> p c t i", i=4)
             src = raw[j][:].rearrange("p t (c i) -> p c t i", i=4)
             v_end = V_COLS // 4
+            g_end = (V_COLS + G_COLS) // 4
             nc.vector.tensor_copy(out=dst[:, :v_end], in_=src[:, :v_end])
-            nc.scalar.copy(out=dst[:, v_end:], in_=src[:, v_end:])
+            nc.gpsimd.tensor_scalar(
+                out=dst[:, v_end:g_end],
+                in0=src[:, v_end:g_end],
+                scalar1=1.0,
+                scalar2=0.0,
+                op0=mybir.AluOpType.mult,
+                op1=mybir.AluOpType.add,
+            )
+            nc.scalar.copy(out=dst[:, g_end:], in_=src[:, g_end:])
             grouped[j] = quads
 
         def quantise(j):

@@ -48,6 +48,7 @@ def tile_selfattention3d_pb_t_kernel(
         work = ctx.enter_context(tc.tile_pool(name="work", bufs=3))
         psum_acc = ctx.enter_context(tc.psum_pool(name="psum_acc", bufs=5))
         psum_tr = ctx.enter_context(tc.psum_pool(name="psum_tr", bufs=3))
+        ctx.enter_context(tc.manual_schedule())
 
         raw = {}
         grouped = {}
@@ -235,7 +236,7 @@ def tile_selfattention3d_pb_t_kernel(
         regroup(2)
         quantise(1)
 
-        for h in range(CHUNKS + 1):
+        for h in range(CHUNKS + 2):
             if h + LOADS_AHEAD < X_TILES:
                 load(h + LOADS_AHEAD)
             if h + 3 < X_TILES:
@@ -244,9 +245,9 @@ def tile_selfattention3d_pb_t_kernel(
                 quantise(h + 2)
             if h < CHUNKS:
                 convolve(h // 2, h % 2)
-            if h > 0:
+            if 0 < h <= CHUNKS:
                 store_theta((h - 1) // 2, (h - 1) % 2)
-                if h % 2 == 0:
-                    store_pooled((h - 1) // 2)
-            if h % 2 == 1:
-                activate_pooled(h // 2)
+            if h >= 2 and h % 2 == 0:
+                activate_pooled((h - 2) // 2)
+            if h >= 3 and h % 2 == 1:
+                store_pooled((h - 3) // 2)

from contextlib import ExitStack

import concourse.mybir as mybir
from concourse.masks import make_identity

BF16 = mybir.dt.bfloat16
F32 = mybir.dt.float32
U32 = mybir.dt.uint32
U8 = mybir.dt.uint8
FP8X4 = mybir.dt.float8_e4m3fn_x4
ACT = mybir.ActivationFunctionType

P = 128
PACK = 4
K_PASS = P * PACK
BATCH = 2
CH = 1024
PASSES = CH // K_PASS
LOCS = 16 * 16 * 16
SLAB = 1024
CHUNK = 512
SLABS_PER_BATCH = LOCS // SLAB
X_TILES = BATCH * SLABS_PER_BATCH * PASSES
CHUNKS = BATCH * LOCS // CHUNK
OUT_TILES = 4
POOLED_TILES = 3
THETA = 3
POOLED = SLAB // 4
V_COLS = 360
G_COLS = 256

LOADS_AHEAD = 6

FLOPS = 2 * BATCH * LOCS * CH * OUT_TILES * P


def tile_selfattention3d_pb_t_kernel(
    tc, x, w_theta, b_theta, w_phi, b_phi, w_g, b_g, out_0, out_1, out_2
):
    nc = tc.nc
    x_view = x.rearrange("b (g t p) f i j -> b g p t (f i j)", g=PASSES, t=PACK, p=P)

    with ExitStack() as ctx:
        consts = ctx.enter_context(tc.tile_pool(name="consts", bufs=1))
        raw_pool = ctx.enter_context(tc.tile_pool(name="raw", bufs=6))
        grouped_pool = ctx.enter_context(tc.tile_pool(name="grouped", bufs=3))
        mx_pool = ctx.enter_context(tc.tile_pool(name="mx", bufs=6))
        work = ctx.enter_context(tc.tile_pool(name="work", bufs=3))
        psum_acc = ctx.enter_context(tc.psum_pool(name="psum_acc", bufs=5))
        psum_tr = ctx.enter_context(tc.psum_pool(name="psum_tr", bufs=3))
        ctx.enter_context(tc.manual_schedule())

        raw = {}
        grouped = {}
        x_codes = {}
        x_scales = {}
        theta_act = {}
        pooled = {}
        pooled_act = {}

        def load(j):
            s, g = j // PASSES, j % PASSES
            bt, n0 = s // SLABS_PER_BATCH, (s % SLABS_PER_BATCH) * SLAB
            rows = raw_pool.tile([P, PACK, SLAB], BF16)
            nc.sync.dma_start(out=rows[:], in_=x_view[bt, g, :, :, n0 : n0 + SLAB])
            raw[j] = rows

        def regroup(j):
            quads = grouped_pool.tile([P, SLAB, PACK], BF16, align_bytes=64)
            dst = quads[:].rearrange("p (c i) t -> p c t i", i=4)
            src = raw[j][:].rearrange("p t (c i) -> p c t i", i=4)
            v_end = V_COLS // 4
            g_end = (V_COLS + G_COLS) // 4
            nc.vector.tensor_copy(out=dst[:, :v_end], in_=src[:, :v_end])
            nc.gpsimd.tensor_scalar(
                out=dst[:, v_end:g_end],
                in0=src[:, v_end:g_end],
                scalar1=1.0,
                scalar2=0.0,
                op0=mybir.AluOpType.mult,
                op1=mybir.AluOpType.add,
            )
            nc.scalar.copy(out=dst[:, g_end:], in_=src[:, g_end:])
            grouped[j] = quads

        def quantise(j):
            codes = mx_pool.tile([P, SLAB], U32, align_bytes=64)
            scales = mx_pool.tile([P, SLAB], U8, align_bytes=64)
            nc.vector.quantize_mx(
                out=codes[:].bitcast(FP8X4),
                scales=scales[:],
                in_=grouped[j][:].rearrange("p n t -> p (n t)"),
            )
            x_codes[j] = codes
            x_scales[j] = scales

        def convolve(s, u):
            cols = slice(u * CHUNK, (u + 1) * CHUNK)
            if u == 0:
                pooled[s] = work.tile([P, POOLED_TILES, POOLED], F32, name="pooled_max")
            for o in range(OUT_TILES):
                outs = slice(o * P, (o + 1) * P)
                acc = psum_acc.tile([P, CHUNK], F32)
                for g in range(PASSES):
                    nc.tensor.matmul_mx(
                        out=acc[:],
                        lhsT=w_codes[:, g, outs].bitcast(FP8X4),
                        lhsT_scale=w_scales[:, g, outs],
                        rhs=x_codes[PASSES * s + g][:, cols].bitcast(FP8X4),
                        rhs_scale=x_scales[PASSES * s + g][:, cols],
                        start=(g == 0),
                        stop=(g == PASSES - 1),
                    )
                if o < POOLED_TILES:
                    nc.vector.tensor_reduce(
                        out=pooled[s][:, o, u * P : (u + 1) * P].rearrange(
                            "p (r j) -> p r j", j=8
                        ),
                        in_=acc[:].rearrange("p (r a j b) -> p r j a b", a=2, j=8, b=2),
                        axis=mybir.AxisListType.XY,
                        op=mybir.AluOpType.max,
                    )
                else:
                    th = work.tile([P, 4, P], F32, name="th")
                    nc.scalar.activation(
                        out=th[:],
                        in_=acc[:].rearrange("p (q r) -> p r q", r=4),
                        func=ACT.Tanh,
                        bias=bias_col[:, THETA : THETA + 1],
                    )
                    theta_act[(s, u)] = th

        def store_theta(s, u):
            bt = s // SLABS_PER_BATCH
            n0 = (s % SLABS_PER_BATCH) * SLAB + u * CHUNK
            th_t = psum_tr.tile([P, 4, P], F32, tag="tr")
            for r in range(4):
                nc.tensor.transpose(th_t[:, r, :], theta_act[(s, u)][:, r, :], ident_f32[:])
            th_out = work.tile([P, 4, P], F32)
            nc.scalar.copy(out=th_out[:], in_=th_t[:])
            nc.sync.dma_start(
                out=out_0[bt, n0 : n0 + CHUNK, :].rearrange("(q r) c -> q r c", r=4),
                in_=th_out[:],
            )

        def activate_pooled(s):
            acted = work.tile([P, POOLED_TILES, 2, P], F32)
            for o in range(POOLED_TILES):
                nc.scalar.activation(
                    out=acted[:, o, :, :],
                    in_=pooled[s][:, o, :].rearrange("p (q r) -> p r q", r=2),
                    func=(ACT.Tanh if o == 0 else ACT.Identity),
                    bias=bias_col[:, o : o + 1],
                )
            pooled_act[s] = acted

        def store_pooled(s):
            bt = s // SLABS_PER_BATCH
            m0 = (s % SLABS_PER_BATCH) * POOLED
            phi_t = psum_tr.tile([P, 2, P], F32, tag="tr")
            g_t = psum_tr.tile([P, 2, 2, P], F32, tag="tr")
            for r in range(2):
                nc.tensor.transpose(phi_t[:, r, :], pooled_act[s][:, 0, r, :], ident_f32[:])
                for h in range(2):
                    nc.tensor.transpose(
                        g_t[:, r, h, :], pooled_act[s][:, 1 + h, r, :], ident_f32[:]
                    )
            phi_out = work.tile([P, 2, P], F32)
            nc.scalar.copy(out=phi_out[:], in_=phi_t[:])
            g_out = work.tile([P, 2, 2 * P], F32)
            nc.scalar.copy(out=g_out[:], in_=g_t[:].rearrange("p r h c -> p r (h c)"))
            nc.sync.dma_start(
                out=out_1[bt, m0 : m0 + POOLED, :].rearrange("(q r) c -> q r c", r=2),
                in_=phi_out[:],
            )
            nc.sync.dma_start(
                out=out_2[bt, m0 : m0 + POOLED, :].rearrange("(q r) c -> q r c", r=2),
                in_=g_out[:],
            )

        load(0)
        load(1)
        w_rows = consts.tile([P, OUT_TILES, CH], BF16)
        nc.sync.dma_start(out=w_rows[:, 0, :], in_=w_phi)
        nc.sync.dma_start(out=w_rows[:, 1:3, :], in_=w_g.rearrange("(h o) k -> o h k", h=2))
        nc.sync.dma_start(out=w_rows[:, THETA, :], in_=w_theta)
        for j in range(2, LOADS_AHEAD):
            load(j)

        bias_rows = consts.tile([P, P], BF16)
        nc.vector.memset(bias_rows[:], 0.0)
        nc.scalar.dma_start(out=bias_rows[0:1, :], in_=b_phi.rearrange("(h c) -> h c", h=1))
        nc.scalar.dma_start(out=bias_rows[1:3, :], in_=b_g.rearrange("(h c) -> h c", h=2))
        nc.scalar.dma_start(
            out=bias_rows[THETA : THETA + 1, :], in_=b_theta.rearrange("(h c) -> h c", h=1)
        )
        ident_bf = consts.tile([P, P], BF16)
        make_identity(nc, ident_bf[:])
        ident_f32 = consts.tile([P, P], F32)
        make_identity(nc, ident_f32[:])

        regroup(0)
        regroup(1)

        w_grouped = consts.tile([P, PASSES, OUT_TILES * P, PACK], BF16, align_bytes=64)
        w_codes = consts.tile([P, PASSES, OUT_TILES * P], U32, align_bytes=64)
        w_scales = consts.tile([P, PASSES, OUT_TILES * P], U8, align_bytes=64)
        for g in range(PASSES):
            for h in range(2):
                w_t = psum_tr.tile([P, 2, PACK, P], BF16, tag="tr")
                for o in range(2):
                    for t in range(PACK):
                        k0 = g * K_PASS + t * P
                        nc.tensor.transpose(
                            w_t[:, o, t, :], w_rows[:, 2 * h + o, k0 : k0 + P], ident_bf[:]
                        )
                dst = w_grouped[:, g, 2 * h * P : (2 * h + 2) * P, :].rearrange(
                    "p (o r) t -> p o r t", o=2
                )
                src = w_t[:].rearrange("p o t r -> p o r t")
                if h == 0:
                    nc.vector.tensor_copy(out=dst, in_=src)
                else:
                    nc.scalar.copy(out=dst, in_=src)
        bias_t = psum_tr.tile([P, P], BF16, tag="tr")
        nc.tensor.transpose(bias_t[:], bias_rows[:], ident_bf[:])
        bias_col = consts.tile([P, OUT_TILES], F32)
        nc.vector.tensor_copy(out=bias_col[:], in_=bias_t[:, 0:OUT_TILES])
        for g in range(PASSES):
            nc.vector.quantize_mx(
                out=w_codes[:, g, :].bitcast(FP8X4),
                scales=w_scales[:, g, :],
                in_=w_grouped[:, g, :, :].rearrange("p r t -> p (r t)"),
            )
        quantise(0)
        regroup(2)
        quantise(1)

        for h in range(CHUNKS + 2):
            if h + LOADS_AHEAD < X_TILES:
                load(h + LOADS_AHEAD)
            if h + 3 < X_TILES:
                regroup(h + 3)
            if h + 2 < X_TILES:
                quantise(h + 2)
            if h < CHUNKS:
                convolve(h // 2, h % 2)
            if 0 < h <= CHUNKS:
                store_theta((h - 1) // 2, (h - 1) % 2)
            if h >= 2 and h % 2 == 0:
                activate_pooled((h - 2) // 2)
            if h >= 3 and h % 2 == 1:
                store_pooled((h - 3) // 2)
